import numpy as np
import ml_dtypes

BF16 = ml_dtypes.bfloat16


def bf(x):
    return np.asarray(x, np.float32).astype(BF16)


def f32(x):
    return np.asarray(x, np.float32)


def f64(x):
    return np.asarray(x).astype(np.float64)


def striped(idx):
    return np.tile(idx.reshape(-1, 16).T, (8, 1))


C, S, N, T, R, M = 128, 2048, 4096, 32, 128, 128


def pos_table():
    t = np.arange(T, dtype=np.float64)[:, None]
    div = np.exp(-np.arange(0, C, 2, dtype=np.float64) * (np.log(10000.0) / C))
    ang = t * div
    pe = np.zeros((T, C))
    pe[:, 0::2] = np.sin(ang)
    pe[:, 1::2] = np.cos(ang)
    return np.repeat(pe.T, R, axis=1)


def setup_inputs():
    return {"emb": f32(np.random.standard_normal((C, S))), "pos": f32(pos_table()), "wm": bf(np.random.standard_normal((T, C, M)) / np.sqrt(T * C)), "bm": f32(0.1 * np.random.standard_normal((M, 1))), "offs": striped(np.random.permutation(np.tile(np.arange(S), 2))[:N])}


def reference(emb, pos, wm, bm, offs):
    idx = offs[:16].T.reshape(-1)
    x = f64(emb)[:, idx] + f64(pos)
    return np.einsum("tcm,ctr->mr", f64(wm), x.reshape(C, T, R)) + f64(bm)

@@ -1,0 +1,50 @@
+import concourse.mybir as mybir
+
+C, S, N, T, R, M = 128, 2048, 4096, 32, 128, 128
+FLOPS = 2 * T * C * M * R
+
+F32, BF16, U16 = mybir.dt.float32, mybir.dt.bfloat16, mybir.dt.uint16
+
+PIECE = 512
+N_PIECES = N // PIECE
+T_PER_PIECE = PIECE // R
+
+
+def tile_lshmodel_kernel(tc, emb, pos, wm, bm, offs, out):
+    nc = tc.nc
+    wm_by_channel = wm.rearrange("t c m -> c t m")
+    with (
+        tc.tile_pool(name="held", bufs=1) as held,
+        tc.tile_pool(name="pieces", bufs=N_PIECES) as pieces,
+        tc.psum_pool(name="psum", bufs=1) as psum,
+    ):
+        offsets = held.tile([C, N // 16], U16, name="offsets")
+        nc.sync.dma_start(offsets[:], offs)
+        table = held.tile([C, S], F32, name="table")
+        nc.sync.dma_start(table[:], emb)
+        bias = held.tile([M, 1], F32, name="bias")
+        nc.scalar.dma_start(bias[:], bm)
+
+        acc = psum.tile([M, R], F32, name="acc")
+        for p in range(N_PIECES):
+            pos_piece = pieces.tile([C, PIECE], F32, name="pos_piece")
+            nc.sync.dma_start(pos_piece[:], pos[:, p * PIECE : (p + 1) * PIECE])
+            wm_piece = pieces.tile([C, T_PER_PIECE, M], BF16, name="wm_piece")
+            nc.scalar.dma_start(wm_piece[:], wm_by_channel[:, p * T_PER_PIECE : (p + 1) * T_PER_PIECE, :])
+
+            x_f32 = pieces.tile([C, PIECE], F32, name="x_f32")
+            picked = table[:].indirect(offsets[:, p * (PIECE // 16) : (p + 1) * (PIECE // 16)])
+            nc.vector.tensor_tensor(x_f32[:], picked, pos_piece[:], mybir.AluOpType.add)
+
+            x_bf16 = pieces.tile([C, PIECE], BF16, name="x_bf16")
+            nc.scalar.copy(x_bf16[:], x_f32[:])
+
+            for k in range(T_PER_PIECE):
+                t = p * T_PER_PIECE + k
+                nc.tensor.matmul(
+                    acc[:], wm_piece[:, k, :], x_bf16[:, k * R : (k + 1) * R], start=(t == 0), stop=(t == T - 1)
+                )
+
+        result = held.tile([M, R], F32, name="result")
+        nc.vector.tensor_scalar_add(result[:], acc[:], bias[:, 0:1])
+        nc.sync.dma_start(out, result[:])

@@ -30,7 +30,7 @@ def tile_lshmodel_kernel(tc, emb, pos, wm, bm, offs, out):
             pos_piece = pieces.tile([C, PIECE], F32, name="pos_piece")
             nc.sync.dma_start(pos_piece[:], pos[:, p * PIECE : (p + 1) * PIECE])
             wm_piece = pieces.tile([C, T_PER_PIECE, M], BF16, name="wm_piece")
-            nc.scalar.dma_start(wm_piece[:], wm_by_channel[:, p * T_PER_PIECE : (p + 1) * T_PER_PIECE, :])
+            nc.sync.dma_start(wm_piece[:], wm_by_channel[:, p * T_PER_PIECE : (p + 1) * T_PER_PIECE, :])
 
             x_f32 = pieces.tile([C, PIECE], F32, name="x_f32")
             picked = table[:].indirect(offsets[:, p * (PIECE // 16) : (p + 1) * (PIECE // 16)])

@@ -5,9 +5,9 @@ FLOPS = 2 * T * C * M * R
 
 F32, BF16, U16 = mybir.dt.float32, mybir.dt.bfloat16, mybir.dt.uint16
 
-PIECE = 512
-N_PIECES = N // PIECE
-T_PER_PIECE = PIECE // R
+WIDTHS = [512] * 7 + [256, 128, 128]
+assert sum(WIDTHS) == N and all(width % R == 0 for width in WIDTHS)
+WIDEST = max(WIDTHS)
 
 
 def tile_lshmodel_kernel(tc, emb, pos, wm, bm, offs, out):
@@ -15,7 +15,7 @@ def tile_lshmodel_kernel(tc, emb, pos, wm, bm, offs, out):
     wm_by_channel = wm.rearrange("t c m -> c t m")
     with (
         tc.tile_pool(name="held", bufs=1) as held,
-        tc.tile_pool(name="pieces", bufs=N_PIECES) as pieces,
+        tc.tile_pool(name="pieces", bufs=len(WIDTHS)) as pieces,
         tc.psum_pool(name="psum", bufs=1) as psum,
     ):
         offsets = held.tile([C, N // 16], U16, name="offsets")
@@ -26,24 +26,27 @@ def tile_lshmodel_kernel(tc, emb, pos, wm, bm, offs, out):
         nc.scalar.dma_start(bias[:], bm)
 
         acc = psum.tile([M, R], F32, name="acc")
-        for p in range(N_PIECES):
-            pos_piece = pieces.tile([C, PIECE], F32, name="pos_piece")
-            nc.sync.dma_start(pos_piece[:], pos[:, p * PIECE : (p + 1) * PIECE])
-            wm_piece = pieces.tile([C, T_PER_PIECE, M], BF16, name="wm_piece")
-            nc.sync.dma_start(wm_piece[:], wm_by_channel[:, p * T_PER_PIECE : (p + 1) * T_PER_PIECE, :])
+        first = 0
+        for width in WIDTHS:
+            t_first, t_count = first // R, width // R
+            pos_piece = pieces.tile([C, WIDEST], F32, name="pos_piece")
+            nc.sync.dma_start(pos_piece[:, :width], pos[:, first : first + width])
+            wm_piece = pieces.tile([C, WIDEST // R, M], BF16, name="wm_piece")
+            nc.sync.dma_start(wm_piece[:, :t_count, :], wm_by_channel[:, t_first : t_first + t_count, :])
 
-            x_f32 = pieces.tile([C, PIECE], F32, name="x_f32")
-            picked = table[:].indirect(offsets[:, p * (PIECE // 16) : (p + 1) * (PIECE // 16)])
-            nc.vector.tensor_tensor(x_f32[:], picked, pos_piece[:], mybir.AluOpType.add)
+            x_f32 = pieces.tile([C, WIDEST], F32, name="x_f32")
+            picked = table[:].indirect(offsets[:, first // 16 : (first + width) // 16])
+            nc.vector.tensor_tensor(x_f32[:, :width], picked, pos_piece[:, :width], mybir.AluOpType.add)
 
-            x_bf16 = pieces.tile([C, PIECE], BF16, name="x_bf16")
-            nc.scalar.copy(x_bf16[:], x_f32[:])
+            x_bf16 = pieces.tile([C, WIDEST], BF16, name="x_bf16")
+            nc.scalar.copy(x_bf16[:, :width], x_f32[:, :width])
 
-            for k in range(T_PER_PIECE):
-                t = p * T_PER_PIECE + k
+            for k in range(t_count):
+                t = t_first + k
                 nc.tensor.matmul(
                     acc[:], wm_piece[:, k, :], x_bf16[:, k * R : (k + 1) * R], start=(t == 0), stop=(t == T - 1)
                 )
+            first += width
 
         result = held.tile([M, R], F32, name="result")
         nc.vector.tensor_scalar_add(result[:], acc[:], bias[:, 0:1])

@@ -7,7 +7,7 @@ F32, BF16, U16 = mybir.dt.float32, mybir.dt.bfloat16, mybir.dt.uint16
 
 WIDTHS = [512] * 7 + [256, 128, 128]
 assert sum(WIDTHS) == N and all(width % R == 0 for width in WIDTHS)
-WIDEST = max(WIDTHS)
+FIRSTS = [sum(WIDTHS[:p]) for p in range(len(WIDTHS))]
 
 
 def tile_lshmodel_kernel(tc, emb, pos, wm, bm, offs, out):
@@ -24,29 +24,31 @@ def tile_lshmodel_kernel(tc, emb, pos, wm, bm, offs, out):
         nc.sync.dma_start(table[:], emb)
         bias = held.tile([M, 1], F32, name="bias")
         nc.scalar.dma_start(bias[:], bm)
+        pos_pieces = []
+        for first, width in zip(FIRSTS, WIDTHS):
+            pos_piece = held.tile([C, width], F32, name=f"pos_{first}")
+            nc.sync.dma_start(pos_piece[:], pos[:, first : first + width])
+            pos_pieces.append(pos_piece)
+        wm_pieces = []
+        for first, width in zip(FIRSTS, WIDTHS):
+            wm_piece = held.tile([C, width // R, M], BF16, name=f"wm_{first}")
+            nc.sync.dma_start(wm_piece[:], wm_by_channel[:, first // R : (first + width) // R, :])
+            wm_pieces.append(wm_piece)
 
         acc = psum.tile([M, R], F32, name="acc")
-        first = 0
-        for width in WIDTHS:
-            t_first, t_count = first // R, width // R
-            pos_piece = pieces.tile([C, WIDEST], F32, name="pos_piece")
-            nc.sync.dma_start(pos_piece[:, :width], pos[:, first : first + width])
-            wm_piece = pieces.tile([C, WIDEST // R, M], BF16, name="wm_piece")
-            nc.sync.dma_start(wm_piece[:, :t_count, :], wm_by_channel[:, t_first : t_first + t_count, :])
-
-            x_f32 = pieces.tile([C, WIDEST], F32, name="x_f32")
+        for first, width, pos_piece, wm_piece in zip(FIRSTS, WIDTHS, pos_pieces, wm_pieces):
+            x_f32 = pieces.tile([C, max(WIDTHS)], F32, name="x_f32")
             picked = table[:].indirect(offsets[:, first // 16 : (first + width) // 16])
-            nc.vector.tensor_tensor(x_f32[:, :width], picked, pos_piece[:, :width], mybir.AluOpType.add)
+            nc.vector.tensor_tensor(x_f32[:, :width], picked, pos_piece[:], mybir.AluOpType.add)
 
-            x_bf16 = pieces.tile([C, WIDEST], BF16, name="x_bf16")
+            x_bf16 = pieces.tile([C, max(WIDTHS)], BF16, name="x_bf16")
             nc.scalar.copy(x_bf16[:, :width], x_f32[:, :width])
 
-            for k in range(t_count):
-                t = t_first + k
+            for k in range(width // R):
+                t = first // R + k
                 nc.tensor.matmul(
                     acc[:], wm_piece[:, k, :], x_bf16[:, k * R : (k + 1) * R], start=(t == 0), stop=(t == T - 1)
                 )
-            first += width
 
         result = held.tile([M, R], F32, name="result")
         nc.vector.tensor_scalar_add(result[:], acc[:], bias[:, 0:1])

@@ -5,7 +5,7 @@ FLOPS = 2 * T * C * M * R
 
 F32, BF16, U16 = mybir.dt.float32, mybir.dt.bfloat16, mybir.dt.uint16
 
-WIDTHS = [512] * 7 + [256, 128, 128]
+WIDTHS = [128, 128, 256] + [512] * 6 + [256, 128, 128]
 assert sum(WIDTHS) == N and all(width % R == 0 for width in WIDTHS)
 FIRSTS = [sum(WIDTHS[:p]) for p in range(len(WIDTHS))]
 

@@ -22,13 +22,13 @@ def tile_lshmodel_kernel(tc, emb, pos, wm, bm, offs, out):
         nc.sync.dma_start(offsets[:], offs)
         table = held.tile([C, S], F32, name="table")
         nc.sync.dma_start(table[:], emb)
-        bias = held.tile([M, 1], F32, name="bias")
-        nc.scalar.dma_start(bias[:], bm)
         pos_pieces = []
         for first, width in zip(FIRSTS, WIDTHS):
             pos_piece = held.tile([C, width], F32, name=f"pos_{first}")
             nc.sync.dma_start(pos_piece[:], pos[:, first : first + width])
             pos_pieces.append(pos_piece)
+        bias = held.tile([M, 1], F32, name="bias")
+        nc.sync.dma_start(bias[:], bm)
         wm_pieces = []
         for first, width in zip(FIRSTS, WIDTHS):
             wm_piece = held.tile([C, width // R, M], BF16, name=f"wm_{first}")

@@ -21,7 +21,8 @@ def tile_lshmodel_kernel(tc, emb, pos, wm, bm, offs, out):
         offsets = held.tile([C, N // 16], U16, name="offsets")
         nc.sync.dma_start(offsets[:], offs)
         table = held.tile([C, S], F32, name="table")
-        nc.sync.dma_start(table[:], emb)
+        nc.sync.dma_start(table[:, : S // 2], emb[:, : S // 2])
+        nc.scalar.dma_start(table[:, S // 2 :], emb[:, S // 2 :])
         pos_pieces = []
         for first, width in zip(FIRSTS, WIDTHS):
             pos_piece = held.tile([C, width], F32, name=f"pos_{first}")

@@ -43,7 +43,10 @@ def tile_lshmodel_kernel(tc, emb, pos, wm, bm, offs, out):
             nc.vector.tensor_tensor(x_f32[:, :width], picked, pos_piece[:], mybir.AluOpType.add)
 
             x_bf16 = pieces.tile([C, max(WIDTHS)], BF16, name="x_bf16")
-            nc.scalar.copy(x_bf16[:, :width], x_f32[:, :width])
+            if first + width < N:
+                nc.scalar.copy(x_bf16[:, :width], x_f32[:, :width])
+            else:
+                nc.vector.tensor_copy(x_bf16[:, :width], x_f32[:, :width])
 
             for k in range(width // R):
                 t = first // R + k

@@ -28,13 +28,13 @@ def tile_lshmodel_kernel(tc, emb, pos, wm, bm, offs, out):
             pos_piece = held.tile([C, width], F32, name=f"pos_{first}")
             nc.sync.dma_start(pos_piece[:], pos[:, first : first + width])
             pos_pieces.append(pos_piece)
-        bias = held.tile([M, 1], F32, name="bias")
-        nc.sync.dma_start(bias[:], bm)
         wm_pieces = []
         for first, width in zip(FIRSTS, WIDTHS):
             wm_piece = held.tile([C, width // R, M], BF16, name=f"wm_{first}")
             nc.sync.dma_start(wm_piece[:], wm_by_channel[:, first // R : (first + width) // R, :])
             wm_pieces.append(wm_piece)
+        bias = held.tile([M, 1], F32, name="bias")
+        nc.sync.dma_start(bias[:], bm)
 
         acc = psum.tile([M, R], F32, name="acc")
         for first, width, pos_piece, wm_piece in zip(FIRSTS, WIDTHS, pos_pieces, wm_pieces):

@@ -5,9 +5,14 @@ FLOPS = 2 * T * C * M * R
 
 F32, BF16, U16 = mybir.dt.float32, mybir.dt.bfloat16, mybir.dt.uint16
 
-WIDTHS = [128, 128, 256] + [512] * 6 + [256, 128, 128]
+WIDTHS = [128, 256, 512, 1024, 1024, 512, 256, 256, 128]
 assert sum(WIDTHS) == N and all(width % R == 0 for width in WIDTHS)
 FIRSTS = [sum(WIDTHS[:p]) for p in range(len(WIDTHS))]
+
+ROUNDED = 256
+
+POSITIONS = [1, 1, 2] + [4] * 7
+assert sum(POSITIONS) == T
 
 
 def tile_lshmodel_kernel(tc, emb, pos, wm, bm, offs, out):
@@ -28,31 +33,34 @@ def tile_lshmodel_kernel(tc, emb, pos, wm, bm, offs, out):
             pos_piece = held.tile([C, width], F32, name=f"pos_{first}")
             nc.sync.dma_start(pos_piece[:], pos[:, first : first + width])
             pos_pieces.append(pos_piece)
-        wm_pieces = []
-        for first, width in zip(FIRSTS, WIDTHS):
-            wm_piece = held.tile([C, width // R, M], BF16, name=f"wm_{first}")
-            nc.sync.dma_start(wm_piece[:], wm_by_channel[:, first // R : (first + width) // R, :])
-            wm_pieces.append(wm_piece)
+        weights = []
+        for count in POSITIONS:
+            t = len(weights)
+            wm_piece = held.tile([C, count, M], BF16, name=f"wm_{t}")
+            nc.sync.dma_start(wm_piece[:], wm_by_channel[:, t : t + count, :])
+            weights.extend(wm_piece[:, k, :] for k in range(count))
         bias = held.tile([M, 1], F32, name="bias")
         nc.sync.dma_start(bias[:], bm)
 
         acc = psum.tile([M, R], F32, name="acc")
-        for first, width, pos_piece, wm_piece in zip(FIRSTS, WIDTHS, pos_pieces, wm_pieces):
+        for first, width, pos_piece in zip(FIRSTS, WIDTHS, pos_pieces):
             x_f32 = pieces.tile([C, max(WIDTHS)], F32, name="x_f32")
             picked = table[:].indirect(offsets[:, first // 16 : (first + width) // 16])
             nc.vector.tensor_tensor(x_f32[:, :width], picked, pos_piece[:], mybir.AluOpType.add)
 
             x_bf16 = pieces.tile([C, max(WIDTHS)], BF16, name="x_bf16")
-            if first + width < N:
-                nc.scalar.copy(x_bf16[:, :width], x_f32[:, :width])
-            else:
-                nc.vector.tensor_copy(x_bf16[:, :width], x_f32[:, :width])
+            for begin in range(0, width, ROUNDED):
+                end = min(begin + ROUNDED, width)
+                if first + width < N:
+                    nc.scalar.copy(x_bf16[:, begin:end], x_f32[:, begin:end])
+                else:
+                    nc.vector.tensor_copy(x_bf16[:, begin:end], x_f32[:, begin:end])
 
-            for k in range(width // R):
-                t = first // R + k
-                nc.tensor.matmul(
-                    acc[:], wm_piece[:, k, :], x_bf16[:, k * R : (k + 1) * R], start=(t == 0), stop=(t == T - 1)
-                )
+                for column in range(begin, end, R):
+                    t = (first + column) // R
+                    nc.tensor.matmul(
+                        acc[:], weights[t], x_bf16[:, column : column + R], start=(t == 0), stop=(t == T - 1)
+                    )
 
         result = held.tile([M, R], F32, name="result")
         nc.vector.tensor_scalar_add(result[:], acc[:], bias[:, 0:1])

@@ -11,7 +11,7 @@ FIRSTS = [sum(WIDTHS[:p]) for p in range(len(WIDTHS))]
 
 ROUNDED = 256
 
-POSITIONS = [1, 1, 2] + [4] * 7
+POSITIONS = [1, 1, 2, 2, 2] + [4] * 6
 assert sum(POSITIONS) == T
 
 
@@ -26,8 +26,7 @@ def tile_lshmodel_kernel(tc, emb, pos, wm, bm, offs, out):
         offsets = held.tile([C, N // 16], U16, name="offsets")
         nc.sync.dma_start(offsets[:], offs)
         table = held.tile([C, S], F32, name="table")
-        nc.sync.dma_start(table[:, : S // 2], emb[:, : S // 2])
-        nc.scalar.dma_start(table[:, S // 2 :], emb[:, S // 2 :])
+        nc.sync.dma_start(table[:], emb)
         pos_pieces = []
         for first, width in zip(FIRSTS, WIDTHS):
             pos_piece = held.tile([C, width], F32, name=f"pos_{first}")

@@ -5,13 +5,13 @@ FLOPS = 2 * T * C * M * R
 
 F32, BF16, U16 = mybir.dt.float32, mybir.dt.bfloat16, mybir.dt.uint16
 
-WIDTHS = [128, 256, 512, 1024, 1024, 512, 256, 256, 128]
+WIDTHS = [128, 256, 512, 1152, 1152, 512, 256, 128]
 assert sum(WIDTHS) == N and all(width % R == 0 for width in WIDTHS)
 FIRSTS = [sum(WIDTHS[:p]) for p in range(len(WIDTHS))]
 
 ROUNDED = 256
 
-POSITIONS = [1, 1, 2, 2, 2] + [4] * 6
+POSITIONS = [1, 1, 1, 1, 2, 2] + [4] * 6
 assert sum(POSITIONS) == T
 
 

@@ -9,6 +9,8 @@ WIDTHS = [128, 256, 512, 1152, 1152, 512, 256, 128]
 assert sum(WIDTHS) == N and all(width % R == 0 for width in WIDTHS)
 FIRSTS = [sum(WIDTHS[:p]) for p in range(len(WIDTHS))]
 
+WORDS = 16
+
 ROUNDED = 256
 
 POSITIONS = [1, 1, 1, 1, 2, 2] + [4] * 6
@@ -26,9 +28,13 @@ def tile_lshmodel_kernel(tc, emb, pos, wm, bm, offs, out):
         offsets = held.tile([C, N // 16], U16, name="offsets")
         nc.sync.dma_start(offsets[:], offs)
         table = held.tile([C, S], F32, name="table")
+        pos_word = held.tile([C, WORDS], F32, name="pos_word")
+        nc.sync.dma_start(pos_word[:], pos[:, :WORDS])
         nc.sync.dma_start(table[:], emb)
-        pos_pieces = []
-        for first, width in zip(FIRSTS, WIDTHS):
+        pos_piece = held.tile([C, R], F32, name="pos_0")
+        nc.vector.tensor_copy(pos_piece[:], pos_word[:, 0:1].to_broadcast([C, R]))
+        pos_pieces = [pos_piece]
+        for first, width in zip(FIRSTS[1:], WIDTHS[1:]):
             pos_piece = held.tile([C, width], F32, name=f"pos_{first}")
             nc.sync.dma_start(pos_piece[:], pos[:, first : first + width])
             pos_pieces.append(pos_piece)

import concourse.mybir as mybir

C, S, N, T, R, M = 128, 2048, 4096, 32, 128, 128
FLOPS = 2 * T * C * M * R

F32, BF16, U16 = mybir.dt.float32, mybir.dt.bfloat16, mybir.dt.uint16

WIDTHS = [128, 256, 512, 1152, 1152, 512, 256, 128]
assert sum(WIDTHS) == N and all(width % R == 0 for width in WIDTHS)
FIRSTS = [sum(WIDTHS[:p]) for p in range(len(WIDTHS))]

WORDS = 16

ROUNDED = 256

POSITIONS = [1, 1, 1, 1, 2, 2] + [4] * 6
assert sum(POSITIONS) == T


def tile_lshmodel_kernel(tc, emb, pos, wm, bm, offs, out):
    nc = tc.nc
    wm_by_channel = wm.rearrange("t c m -> c t m")
    with (
        tc.tile_pool(name="held", bufs=1) as held,
        tc.tile_pool(name="pieces", bufs=len(WIDTHS)) as pieces,
        tc.psum_pool(name="psum", bufs=1) as psum,
    ):
        offsets = held.tile([C, N // 16], U16, name="offsets")
        nc.sync.dma_start(offsets[:], offs)
        table = held.tile([C, S], F32, name="table")
        pos_word = held.tile([C, WORDS], F32, name="pos_word")
        nc.sync.dma_start(pos_word[:], pos[:, :WORDS])
        nc.sync.dma_start(table[:], emb)
        pos_piece = held.tile([C, R], F32, name="pos_0")
        nc.vector.tensor_copy(pos_piece[:], pos_word[:, 0:1].to_broadcast([C, R]))
        pos_pieces = [pos_piece]
        for first, width in zip(FIRSTS[1:], WIDTHS[1:]):
            pos_piece = held.tile([C, width], F32, name=f"pos_{first}")
            nc.sync.dma_start(pos_piece[:], pos[:, first : first + width])
            pos_pieces.append(pos_piece)
        weights = []
        for count in POSITIONS:
            t = len(weights)
            wm_piece = held.tile([C, count, M], BF16, name=f"wm_{t}")
            nc.sync.dma_start(wm_piece[:], wm_by_channel[:, t : t + count, :])
            weights.extend(wm_piece[:, k, :] for k in range(count))
        bias = held.tile([M, 1], F32, name="bias")
        nc.sync.dma_start(bias[:], bm)

        acc = psum.tile([M, R], F32, name="acc")
        for first, width, pos_piece in zip(FIRSTS, WIDTHS, pos_pieces):
            x_f32 = pieces.tile([C, max(WIDTHS)], F32, name="x_f32")
            picked = table[:].indirect(offsets[:, first // 16 : (first + width) // 16])
            nc.vector.tensor_tensor(x_f32[:, :width], picked, pos_piece[:], mybir.AluOpType.add)

            x_bf16 = pieces.tile([C, max(WIDTHS)], BF16, name="x_bf16")
            for begin in range(0, width, ROUNDED):
                end = min(begin + ROUNDED, width)
                if first + width < N:
                    nc.scalar.copy(x_bf16[:, begin:end], x_f32[:, begin:end])
                else:
                    nc.vector.tensor_copy(x_bf16[:, begin:end], x_f32[:, begin:end])

                for column in range(begin, end, R):
                    t = (first + column) // R
                    nc.tensor.matmul(
                        acc[:], weights[t], x_bf16[:, column : column + R], start=(t == 0), stop=(t == T - 1)
                    )

        result = held.tile([M, R], F32, name="result")
        nc.vector.tensor_scalar_add(result[:], acc[:], bias[:, 0:1])
        nc.sync.dma_start(out, result[:])
